import numpy as np
import ml_dtypes


def mxq(x, axis, fmt="e4m3"):
    dtype, down = {"e4m3": (ml_dtypes.float8_e4m3fn, 7), "e5m2": (ml_dtypes.float8_e5m2, 14)}[fmt]
    v = np.moveaxis(np.asarray(x, np.float32).astype(ml_dtypes.bfloat16).astype(np.float64), axis, -1)
    blocks = v.reshape(v.shape[:-1] + (-1, 32))
    amax = np.abs(blocks).max(-1, keepdims=True)
    byte = np.maximum(np.where(amax > 0, np.frexp(amax)[1] - 1 + 127, 0) - down, 1)
    scale = np.exp2(byte - 127.0)
    codes = (blocks / scale).astype(np.float32).astype(dtype).astype(np.float64)
    return np.moveaxis((codes * scale).reshape(v.shape), -1, axis)


WIDE = False


def mx_kscale(k):
    if not WIDE:
        return np.ones(k)
    levels = np.array([10, -10, 5, -5, 0])
    a = np.random.permutation(np.resize(levels, k // 512 * 4)).reshape(k // 512, 4)
    idx = np.arange(k)
    return np.exp2(a[idx // 512, idx % 128 // 32])


BF16 = ml_dtypes.bfloat16


def bf(x):
    return np.asarray(x, np.float32).astype(BF16)


def f64(x):
    return np.asarray(x).astype(np.float64)


B, I0, I1, I2, O0, O1, O2, R1, R2 = 4096, 128, 8, 4, 1, 1, 128, 128, 128


def pos(lo, *shape):
    return np.random.uniform(lo, 2.0 - lo, shape)


def setup_inputs():
    a1 = mx_kscale(R1 * I1)[::I1]
    a2 = mx_kscale(R2 * I2)[::I2]
    return {"vector": bf(pos(0.25, B, I0, I1, I2) * pos(0.5, B, 1, I1, I2) * pos(0.5, B, 1, 1, 1)),
            "core0": bf(pos(0.25, 1, O0, I0, R1) * pos(0.5, 1, O0, 1, 1) * pos(0.5, 1, 1, 1, R1) / I0 * a1),
            "core1": bf(pos(0.25, R1, O1, I1, R2) * pos(0.5, 1, O1, 1, 1) * pos(0.5, 1, 1, 1, R2) / (R1 * I1) / a1[:, None, None, None] * a2),
            "core2": bf(pos(0.25, R2, O2, I2, 1) * pos(0.5, 1, O2, 1, 1) / (R2 * I2) / a2[:, None, None, None])}


def _contract(res, bs, core, quantised):
    r, o, i, k = core.shape
    rem = res.shape[3:]
    a = res.reshape(bs, r * i, -1)
    x = a.shape[2]
    a = a.transpose(0, 2, 1).reshape(bs * x, r * i)
    w = core.transpose(0, 2, 1, 3).reshape(r * i, o * k)
    if quantised:
        y = mxq(a, 1, "e4m3") @ mxq(w, 0, "e4m3")
    else:
        y = a @ w
    y = y.reshape(bs, x, o, k).transpose(0, 2, 3, 1)
    return y.reshape(bs * o, k, *rem), bs * o


def reference(vector, core0, core1, core2):
    bs0 = vector.shape[0]
    res = f64(vector)[:, None]
    bs = bs0
    res, bs = _contract(res, bs, f64(core0), False)
    res, bs = _contract(res, bs, f64(core1), True)
    res, bs = _contract(res, bs, f64(core2), True)
    res = np.squeeze(res, axis=-1)
    return res.reshape(bs0, core0.shape[1], core1.shape[1], core2.shape[1])

@@ -1,0 +1,226 @@
+from contextlib import ExitStack
+
+import concourse.mybir as mybir
+from concourse.masks import make_identity
+
+BF16 = mybir.dt.bfloat16
+F32 = mybir.dt.float32
+U32 = mybir.dt.uint32
+U8 = mybir.dt.uint8
+FP8X4 = mybir.dt.float8_e4m3fn_x4
+
+B, I0, I1, I2 = 4096, 128, 8, 4
+R1, R2, O2 = 128, 128, 128
+FLOPS = 2 * B * (I0 * R1 * I1 * I2 + R1 * I1 * R2 * I2 + R2 * I2 * O2)
+
+P = 128
+PACK = 4
+HALVES = I1 // PACK
+PAIRS = I2 // 2
+QUARTERS = HALVES * PAIRS
+WORDS = I1 * PAIRS
+N_TILES = B // P
+COLS = I2 * P
+LOOKAHEAD = 4
+VECTOR_QUARTERS = 3
+MX_QUARTER = 3
+
+
+def rank_order(ap):
+    return ap.rearrange("p (a j c d) -> p j a c d", a=4, j=2, c=4, d=4)
+
+
+def block_order(ap):
+    return ap.rearrange("p (a c j d) -> p j a c d", a=4, c=4, j=2, d=4)
+
+
+def live(n):
+    return 0 <= n < N_TILES
+
+
+def tile_ttmatrix_t_kernel(tc, vector, core0, core1, core2, out):
+    nc = tc.nc
+    x_dram = vector.rearrange("(n b) i j k -> n b (i j k)", b=P)
+    out_dram = out.rearrange("(n b) x y o -> n b (x y o)", b=P)
+
+    with ExitStack() as ctx:
+        consts = ctx.enter_context(tc.tile_pool(name="consts", bufs=1))
+        x_pool = ctx.enter_context(tc.tile_pool(name="x", bufs=LOOKAHEAD + 1))
+        work = ctx.enter_context(tc.tile_pool(name="work", bufs=3))
+        xt_psum = ctx.enter_context(tc.psum_pool(name="xt_psum", bufs=3))
+        h0_psum = ctx.enter_context(tc.psum_pool(name="h0_psum", bufs=3))
+        h1_psum = ctx.enter_context(tc.psum_pool(name="h1_psum", bufs=1))
+        out_psum = ctx.enter_context(tc.psum_pool(name="out_psum", bufs=1))
+        ctx.enter_context(tc.manual_schedule())
+
+        x_tiles, xt_tiles, h0_tiles = {}, {}, {}
+        h0_codes, h0_scales, h1_tiles, h1_codes, h1_scales, out_banks = {}, {}, {}, {}, {}, {}
+
+        def load(n):
+            if live(n):
+                x_sb = x_pool.tile([P, I0 * I1 * I2], BF16)
+                nc.sync.dma_start(out=x_sb[:], in_=x_dram[n])
+                x_tiles[n] = x_sb
+
+        load(0)
+        c0_sb = consts.tile([P, R1], BF16)
+        nc.sync.dma_start(out=c0_sb[:], in_=core0.rearrange("x y i r -> (x y i) r"))
+        c1_sb = consts.tile([P, I1 * R2], BF16)
+        nc.sync.dma_start(out=c1_sb[:], in_=core1.rearrange("r x i s -> r (x i s)"))
+        c2_sb = consts.tile([P, O2 * I2], BF16, align_bytes=64)
+        nc.sync.dma_start(out=c2_sb[:], in_=core2.rearrange("r o i x -> r (o i x)"))
+        for n in range(1, LOOKAHEAD):
+            load(n)
+
+        ident = consts.tile([P, P], F32)
+        make_identity(nc, ident[:])
+        to_block_order = consts.tile([P, P], BF16)
+        for j in range(2):
+            nc.vector.tensor_copy(out=block_order(to_block_order[:])[:, j], in_=rank_order(ident[:])[:, j])
+
+        c0_blocked = consts.tile([P, R1], BF16)
+        c1_grouped = consts.tile([P, HALVES, R2 * PACK], BF16, align_bytes=64)
+        c1_codes = consts.tile([P, HALVES, R2], U32, align_bytes=64)
+        c1_scales = consts.tile([P, HALVES, R2], U8, align_bytes=64)
+        c2_codes = consts.tile([P, O2], U32, align_bytes=64)
+        c2_scales = consts.tile([P, O2], U8, align_bytes=64)
+
+        def prepare_cores():
+            for j in range(2):
+                nc.vector.tensor_copy(out=block_order(c0_blocked[:])[:, j], in_=rank_order(c0_sb[:])[:, j])
+            for h in range(HALVES):
+                xt_bank = xt_psum.tile([P, PACK, P], F32)
+                nc.tensor.matmul(
+                    out=xt_bank[:].rearrange("p t s -> p (t s)"),
+                    lhsT=to_block_order[:],
+                    rhs=c1_sb[:, h * PACK * R2 : (h + 1) * PACK * R2],
+                    start=True,
+                    stop=True,
+                )
+                nc.vector.tensor_copy(
+                    out=c1_grouped[:, h, :].rearrange("p (s t) -> p s t", t=PACK),
+                    in_=xt_bank[:].rearrange("p t s -> p s t"),
+                )
+            nc.vector.quantize_mx(out=c2_codes[:].bitcast(FP8X4), scales=c2_scales[:], in_=c2_sb[:])
+            nc.vector.quantize_mx(
+                out=c1_codes[:].rearrange("p h s -> p (h s)").bitcast(FP8X4),
+                scales=c1_scales[:].rearrange("p h s -> p (h s)"),
+                in_=c1_grouped[:].rearrange("p h c -> p (h c)"),
+            )
+
+        def quarter(n, q):
+            h, u = divmod(q, PAIRS)
+            if live(n):
+                h0_bank = h0_psum.tile([P, 2, P * PACK], BF16)
+            if live(n + 1):
+                xt_bank = xt_psum.tile([P, PACK, P], F32)
+                x_words = x_tiles[n + 1][:].bitcast(F32).rearrange("b (i w) -> b w i", w=WORDS)
+            for e in range(2):
+                if live(n):
+                    nc.tensor.matmul(
+                        out=h0_bank[:, e, :],
+                        lhsT=c0_blocked[:],
+                        rhs=xt_tiles[n][:, q, :].rearrange("p (c e) -> p e c", e=2)[:, e, :],
+                        start=True,
+                        stop=True,
+                    )
+                if live(n + 1):
+                    for t in range(2 * e, 2 * e + 2):
+                        nc.tensor.transpose(
+                            out=xt_bank[:, t, :],
+                            in_=x_words[:, (PACK * h + t) * PAIRS + u, :],
+                            identity=ident[:],
+                        )
+            if live(n):
+                width = 2 * P * PACK
+                nc.scalar.copy(
+                    out=h0_tiles[n][:, h, u * width : (u + 1) * width],
+                    in_=h0_bank[:].rearrange("p e c -> p (e c)"),
+                )
+            if live(n + 1):
+                xt_words = xt_tiles[n + 1][:, q, :].bitcast(F32).rearrange("p (b t) -> p b t", t=PACK)
+                if q < VECTOR_QUARTERS:
+                    nc.vector.tensor_copy(out=xt_words, in_=xt_bank[:].rearrange("p t b -> p b t"))
+                else:
+                    nc.scalar.copy(out=xt_words, in_=xt_bank[:].rearrange("p t b -> p b t"))
+
+        def quantise_h0(n):
+            if live(n):
+                codes = work.tile([P, HALVES, COLS], U32, align_bytes=64)
+                scales = work.tile([P, HALVES, COLS], U8, align_bytes=64)
+                nc.vector.quantize_mx(
+                    out=codes[:].rearrange("p h c -> p (h c)").bitcast(FP8X4),
+                    scales=scales[:].rearrange("p h c -> p (h c)"),
+                    in_=h0_tiles[n][:].rearrange("p h c -> p (h c)"),
+                )
+                h0_codes[n], h0_scales[n] = codes, scales
+
+        def second_contraction(n):
+            if live(n):
+                h1_bank = h1_psum.tile([P, COLS], F32)
+                for h in range(HALVES):
+                    nc.tensor.matmul_mx(
+                        out=h1_bank[:],
+                        lhsT=c1_codes[:, h, :].bitcast(FP8X4),
+                        lhsT_scale=c1_scales[:, h, :],
+                        rhs=h0_codes[n][:, h, :].bitcast(FP8X4),
+                        rhs_scale=h0_scales[n][:, h, :],
+                        start=(h == 0),
+                        stop=(h == HALVES - 1),
+                    )
+                h1_sb = work.tile([P, P, I2], BF16, align_bytes=64)
+                nc.scalar.copy(out=h1_sb[:], in_=h1_bank[:].rearrange("p (i b) -> p b i", i=I2))
+                h1_tiles[n] = h1_sb
+
+        def quantise_h1(n):
+            if live(n):
+                codes2 = work.tile([P, P], U32, align_bytes=64)
+                scales2 = work.tile([P, P], U8, align_bytes=64)
+                nc.vector.quantize_mx(
+                    out=codes2[:].bitcast(FP8X4),
+                    scales=scales2[:],
+                    in_=h1_tiles[n][:].rearrange("p b i -> p (b i)"),
+                )
+                h1_codes[n], h1_scales[n] = codes2, scales2
+
+        def third_contraction(n):
+            if live(n):
+                out_bank = out_psum.tile([P, O2], F32)
+                nc.tensor.matmul_mx(
+                    out=out_bank[:],
+                    lhsT=h1_codes[n][:].bitcast(FP8X4),
+                    lhsT_scale=h1_scales[n][:],
+                    rhs=c2_codes[:].bitcast(FP8X4),
+                    rhs_scale=c2_scales[:],
+                    start=True,
+                    stop=True,
+                )
+                out_banks[n] = out_bank
+
+        def store(n):
+            if live(n):
+                result = work.tile([P, O2], F32)
+                nc.vector.tensor_copy(out=result[:], in_=out_banks[n][:])
+                nc.sync.dma_start(out=out_dram[n], in_=result[:])
+
+        def step(n):
+            if live(n):
+                h0_sb = work.tile([P, HALVES, COLS * PACK], BF16, align_bytes=64)
+                h0_tiles[n] = h0_sb
+            if live(n + 1):
+                xt_sb = work.tile([P, QUARTERS, P * PACK * 2], BF16)
+                xt_tiles[n + 1] = xt_sb
+            quantise_h0(n - 1)
+            for q in range(QUARTERS):
+                if q == MX_QUARTER:
+                    third_contraction(n - 2)
+                    second_contraction(n - 1)
+                quarter(n, q)
+            store(n - 2)
+            quantise_h1(n - 1)
+
+        step(-1)
+        prepare_cores()
+        for n in range(N_TILES + 2):
+            load(n + LOOKAHEAD)
+            step(n)

@@ -23,7 +23,6 @@ N_TILES = B // P
 COLS = I2 * P
 LOOKAHEAD = 4
 VECTOR_QUARTERS = 3
-MX_QUARTER = 3
 
 
 def rank_order(ap):
@@ -144,16 +143,13 @@ def tile_ttmatrix_t_kernel(tc, vector, core0, core1, core2, out):
                 else:
                     nc.scalar.copy(out=xt_words, in_=xt_bank[:].rearrange("p t b -> p b t"))
 
-        def quantise_h0(n):
+        def quantise_h0(n, h):
             if live(n):
-                codes = work.tile([P, HALVES, COLS], U32, align_bytes=64)
-                scales = work.tile([P, HALVES, COLS], U8, align_bytes=64)
                 nc.vector.quantize_mx(
-                    out=codes[:].rearrange("p h c -> p (h c)").bitcast(FP8X4),
-                    scales=scales[:].rearrange("p h c -> p (h c)"),
-                    in_=h0_tiles[n][:].rearrange("p h c -> p (h c)"),
+                    out=h0_codes[n][:, h, :].bitcast(FP8X4),
+                    scales=h0_scales[n][:, h, :],
+                    in_=h0_tiles[n][:, h, :],
                 )
-                h0_codes[n], h0_scales[n] = codes, scales
 
         def second_contraction(n):
             if live(n):
@@ -210,17 +206,23 @@ def tile_ttmatrix_t_kernel(tc, vector, core0, core1, core2, out):
             if live(n + 1):
                 xt_sb = work.tile([P, QUARTERS, P * PACK * 2], BF16)
                 xt_tiles[n + 1] = xt_sb
-            quantise_h0(n - 1)
-            for q in range(QUARTERS):
-                if q == MX_QUARTER:
-                    third_contraction(n - 2)
-                    second_contraction(n - 1)
-                quarter(n, q)
-            store(n - 2)
-            quantise_h1(n - 1)
+            if live(n - 1):
+                codes = work.tile([P, HALVES, COLS], U32, align_bytes=64)
+                scales = work.tile([P, HALVES, COLS], U8, align_bytes=64)
+                h0_codes[n - 1], h0_scales[n - 1] = codes, scales
+            quarter(n, 0)
+            quantise_h0(n - 1, 0)
+            second_contraction(n - 2)
+            third_contraction(n - 3)
+            quarter(n, 1)
+            quantise_h0(n - 1, 1)
+            quarter(n, 2)
+            store(n - 3)
+            quarter(n, 3)
+            quantise_h1(n - 2)
 
         step(-1)
         prepare_cores()
-        for n in range(N_TILES + 2):
+        for n in range(N_TILES + 3):
             load(n + LOOKAHEAD)
             step(n)

@@ -21,6 +21,7 @@ QUARTERS = HALVES * PAIRS
 WORDS = I1 * PAIRS
 N_TILES = B // P
 COLS = I2 * P
+HALF_COLS = P * PACK // 2
 LOOKAHEAD = 4
 VECTOR_QUARTERS = 3
 
@@ -114,22 +115,23 @@ def tile_ttmatrix_t_kernel(tc, vector, core0, core1, core2, out):
             if live(n + 1):
                 xt_bank = xt_psum.tile([P, PACK, P], F32)
                 x_words = x_tiles[n + 1][:].bitcast(F32).rearrange("b (i w) -> b w i", w=WORDS)
-            for e in range(2):
+            for t in range(PACK):
                 if live(n):
+                    e, part = divmod(t, 2)
+                    cols = slice(part * HALF_COLS, (part + 1) * HALF_COLS)
                     nc.tensor.matmul(
-                        out=h0_bank[:, e, :],
+                        out=h0_bank[:, e, cols],
                         lhsT=c0_blocked[:],
-                        rhs=xt_tiles[n][:, q, :].rearrange("p (c e) -> p e c", e=2)[:, e, :],
+                        rhs=xt_tiles[n][:, q, :].rearrange("p (c e) -> p e c", e=2)[:, e, cols],
                         start=True,
                         stop=True,
                     )
                 if live(n + 1):
-                    for t in range(2 * e, 2 * e + 2):
-                        nc.tensor.transpose(
-                            out=xt_bank[:, t, :],
-                            in_=x_words[:, (PACK * h + t) * PAIRS + u, :],
-                            identity=ident[:],
-                        )
+                    nc.tensor.transpose(
+                        out=xt_bank[:, t, :],
+                        in_=x_words[:, (PACK * h + t) * PAIRS + u, :],
+                        identity=ident[:],
+                    )
             if live(n):
                 width = 2 * P * PACK
                 nc.scalar.copy(

@@ -21,9 +21,10 @@ QUARTERS = HALVES * PAIRS
 WORDS = I1 * PAIRS
 N_TILES = B // P
 COLS = I2 * P
-HALF_COLS = P * PACK // 2
 LOOKAHEAD = 4
-VECTOR_QUARTERS = 3
+VECTOR_QUARTERS = 2
+GROUP = 4
+SORTED_GROUPS = 2
 
 
 def rank_order(ap):
@@ -53,7 +54,7 @@ def tile_ttmatrix_t_kernel(tc, vector, core0, core1, core2, out):
         out_psum = ctx.enter_context(tc.psum_pool(name="out_psum", bufs=1))
         ctx.enter_context(tc.manual_schedule())
 
-        x_tiles, xt_tiles, h0_tiles = {}, {}, {}
+        x_tiles, sorted_tiles, xt_tiles, h0_tiles = {}, {}, {}, {}
         h0_codes, h0_scales, h1_tiles, h1_codes, h1_scales, out_banks = {}, {}, {}, {}, {}, {}
 
         def load(n):
@@ -62,14 +63,24 @@ def tile_ttmatrix_t_kernel(tc, vector, core0, core1, core2, out):
                 nc.sync.dma_start(out=x_sb[:], in_=x_dram[n])
                 x_tiles[n] = x_sb
 
-        load(0)
+        def sort_words(n):
+            if live(n):
+                sorted_sb = work.tile([P, SORTED_GROUPS * GROUP, I0], F32)
+                x_words = x_tiles[n][:].bitcast(F32).rearrange("b (i w) -> b i w", w=WORDS)
+                for g in range(SORTED_GROUPS):
+                    words = slice(g * GROUP, (g + 1) * GROUP)
+                    nc.vector.tensor_copy(
+                        out=sorted_sb[:, words, :].rearrange("b w i -> b i w"), in_=x_words[:, :, words]
+                    )
+                sorted_tiles[n] = sorted_sb
+
         c0_sb = consts.tile([P, R1], BF16)
         nc.sync.dma_start(out=c0_sb[:], in_=core0.rearrange("x y i r -> (x y i) r"))
         c1_sb = consts.tile([P, I1 * R2], BF16)
         nc.sync.dma_start(out=c1_sb[:], in_=core1.rearrange("r x i s -> r (x i s)"))
         c2_sb = consts.tile([P, O2 * I2], BF16, align_bytes=64)
         nc.sync.dma_start(out=c2_sb[:], in_=core2.rearrange("r o i x -> r (o i x)"))
-        for n in range(1, LOOKAHEAD):
+        for n in range(LOOKAHEAD):
             load(n)
 
         ident = consts.tile([P, P], F32)
@@ -115,23 +126,22 @@ def tile_ttmatrix_t_kernel(tc, vector, core0, core1, core2, out):
             if live(n + 1):
                 xt_bank = xt_psum.tile([P, PACK, P], F32)
                 x_words = x_tiles[n + 1][:].bitcast(F32).rearrange("b (i w) -> b w i", w=WORDS)
-            for t in range(PACK):
+            for e in range(2):
                 if live(n):
-                    e, part = divmod(t, 2)
-                    cols = slice(part * HALF_COLS, (part + 1) * HALF_COLS)
                     nc.tensor.matmul(
-                        out=h0_bank[:, e, cols],
+                        out=h0_bank[:, e, :],
                         lhsT=c0_blocked[:],
-                        rhs=xt_tiles[n][:, q, :].rearrange("p (c e) -> p e c", e=2)[:, e, cols],
+                        rhs=xt_tiles[n][:, q, :].rearrange("p (c e) -> p e c", e=2)[:, e, :],
                         start=True,
                         stop=True,
                     )
                 if live(n + 1):
-                    nc.tensor.transpose(
-                        out=xt_bank[:, t, :],
-                        in_=x_words[:, (PACK * h + t) * PAIRS + u, :],
-                        identity=ident[:],
-                    )
+                    for t in range(2 * e, 2 * e + 2):
+                        w = (PACK * h + t) * PAIRS + u
+                        if w < SORTED_GROUPS * GROUP:
+                            nc.tensor.transpose(out=xt_bank[:, t, :], in_=sorted_tiles[n + 1][:, w, :], identity=ident[:])
+                        else:
+                            nc.tensor.transpose(out=xt_bank[:, t, :], in_=x_words[:, w, :], identity=ident[:])
             if live(n):
                 width = 2 * P * PACK
                 nc.scalar.copy(
@@ -219,12 +229,14 @@ def tile_ttmatrix_t_kernel(tc, vector, core0, core1, core2, out):
             quarter(n, 1)
             quantise_h0(n - 1, 1)
             quarter(n, 2)
+            sort_words(n + 2)
             store(n - 3)
             quarter(n, 3)
             quantise_h1(n - 2)
 
-        step(-1)
         prepare_cores()
+        sort_words(0)
+        step(-1)
         for n in range(N_TILES + 3):
             load(n + LOOKAHEAD)
             step(n)

@@ -24,7 +24,7 @@ COLS = I2 * P
 LOOKAHEAD = 4
 VECTOR_QUARTERS = 2
 GROUP = 4
-SORTED_GROUPS = 2
+SORTED_GROUPS = (0, 2)
 
 
 def rank_order(ap):
@@ -65,12 +65,12 @@ def tile_ttmatrix_t_kernel(tc, vector, core0, core1, core2, out):
 
         def sort_words(n):
             if live(n):
-                sorted_sb = work.tile([P, SORTED_GROUPS * GROUP, I0], F32)
+                sorted_sb = work.tile([P, len(SORTED_GROUPS) * GROUP, I0], F32)
                 x_words = x_tiles[n][:].bitcast(F32).rearrange("b (i w) -> b i w", w=WORDS)
-                for g in range(SORTED_GROUPS):
-                    words = slice(g * GROUP, (g + 1) * GROUP)
+                for j, g in enumerate(SORTED_GROUPS):
                     nc.vector.tensor_copy(
-                        out=sorted_sb[:, words, :].rearrange("b w i -> b i w"), in_=x_words[:, :, words]
+                        out=sorted_sb[:, j * GROUP : (j + 1) * GROUP, :].rearrange("b w i -> b i w"),
+                        in_=x_words[:, :, g * GROUP : (g + 1) * GROUP],
                     )
                 sorted_tiles[n] = sorted_sb
 
@@ -119,13 +119,10 @@ def tile_ttmatrix_t_kernel(tc, vector, core0, core1, core2, out):
                 in_=c1_grouped[:].rearrange("p h c -> p (h c)"),
             )
 
-        def quarter(n, q):
+        def quarter(n, q, between=()):
             h, u = divmod(q, PAIRS)
             if live(n):
                 h0_bank = h0_psum.tile([P, 2, P * PACK], BF16)
-            if live(n + 1):
-                xt_bank = xt_psum.tile([P, PACK, P], F32)
-                x_words = x_tiles[n + 1][:].bitcast(F32).rearrange("b (i w) -> b w i", w=WORDS)
             for e in range(2):
                 if live(n):
                     nc.tensor.matmul(
@@ -135,13 +132,20 @@ def tile_ttmatrix_t_kernel(tc, vector, core0, core1, core2, out):
                         start=True,
                         stop=True,
                     )
-                if live(n + 1):
-                    for t in range(2 * e, 2 * e + 2):
-                        w = (PACK * h + t) * PAIRS + u
-                        if w < SORTED_GROUPS * GROUP:
-                            nc.tensor.transpose(out=xt_bank[:, t, :], in_=sorted_tiles[n + 1][:, w, :], identity=ident[:])
-                        else:
-                            nc.tensor.transpose(out=xt_bank[:, t, :], in_=x_words[:, w, :], identity=ident[:])
+                if e == 0:
+                    for contraction, tile in between:
+                        contraction(tile)
+            if live(n + 1):
+                xt_bank = xt_psum.tile([P, PACK, P], F32)
+                x_words = x_tiles[n + 1][:].bitcast(F32).rearrange("b (i w) -> b w i", w=WORDS)
+                for t in (2, 3, 0, 1):
+                    w = (PACK * h + t) * PAIRS + u
+                    g, w_in_group = divmod(w, GROUP)
+                    if g in SORTED_GROUPS:
+                        words = sorted_tiles[n + 1][:, SORTED_GROUPS.index(g) * GROUP + w_in_group, :]
+                    else:
+                        words = x_words[:, w, :]
+                    nc.tensor.transpose(out=xt_bank[:, t, :], in_=words, identity=ident[:])
             if live(n):
                 width = 2 * P * PACK
                 nc.scalar.copy(
@@ -224,9 +228,7 @@ def tile_ttmatrix_t_kernel(tc, vector, core0, core1, core2, out):
                 h0_codes[n - 1], h0_scales[n - 1] = codes, scales
             quarter(n, 0)
             quantise_h0(n - 1, 0)
-            second_contraction(n - 2)
-            third_contraction(n - 3)
-            quarter(n, 1)
+            quarter(n, 1, between=((second_contraction, n - 2), (third_contraction, n - 3)))
             quantise_h0(n - 1, 1)
             quarter(n, 2)
             sort_words(n + 2)

@@ -21,7 +21,7 @@ QUARTERS = HALVES * PAIRS
 WORDS = I1 * PAIRS
 N_TILES = B // P
 COLS = I2 * P
-LOOKAHEAD = 4
+LOOKAHEAD = 5
 VECTOR_QUARTERS = 2
 GROUP = 4
 SORTED_GROUPS = (0, 2)
@@ -74,13 +74,14 @@ def tile_ttmatrix_t_kernel(tc, vector, core0, core1, core2, out):
                     )
                 sorted_tiles[n] = sorted_sb
 
+        load(0)
         c0_sb = consts.tile([P, R1], BF16)
         nc.sync.dma_start(out=c0_sb[:], in_=core0.rearrange("x y i r -> (x y i) r"))
         c1_sb = consts.tile([P, I1 * R2], BF16)
         nc.sync.dma_start(out=c1_sb[:], in_=core1.rearrange("r x i s -> r (x i s)"))
         c2_sb = consts.tile([P, O2 * I2], BF16, align_bytes=64)
         nc.sync.dma_start(out=c2_sb[:], in_=core2.rearrange("r o i x -> r (o i x)"))
-        for n in range(LOOKAHEAD):
+        for n in range(1, LOOKAHEAD):
             load(n)
 
         ident = consts.tile([P, P], F32)
@@ -96,9 +97,11 @@ def tile_ttmatrix_t_kernel(tc, vector, core0, core1, core2, out):
         c2_codes = consts.tile([P, O2], U32, align_bytes=64)
         c2_scales = consts.tile([P, O2], U8, align_bytes=64)
 
-        def prepare_cores():
+        def prepare_core0():
             for j in range(2):
                 nc.vector.tensor_copy(out=block_order(c0_blocked[:])[:, j], in_=rank_order(c0_sb[:])[:, j])
+
+        def prepare_core1_and_core2():
             for h in range(HALVES):
                 xt_bank = xt_psum.tile([P, PACK, P], F32)
                 nc.tensor.matmul(
@@ -231,14 +234,17 @@ def tile_ttmatrix_t_kernel(tc, vector, core0, core1, core2, out):
             quarter(n, 1, between=((second_contraction, n - 2), (third_contraction, n - 3)))
             quantise_h0(n - 1, 1)
             quarter(n, 2)
-            sort_words(n + 2)
+            sort_words(n + 3)
             store(n - 3)
             quarter(n, 3)
             quantise_h1(n - 2)
 
-        prepare_cores()
         sort_words(0)
+        prepare_core0()
+        sort_words(1)
         step(-1)
         for n in range(N_TILES + 3):
             load(n + LOOKAHEAD)
             step(n)
+            if n == 0:
+                prepare_core1_and_core2()

from contextlib import ExitStack

import concourse.mybir as mybir
from concourse.masks import make_identity

BF16 = mybir.dt.bfloat16
F32 = mybir.dt.float32
U32 = mybir.dt.uint32
U8 = mybir.dt.uint8
FP8X4 = mybir.dt.float8_e4m3fn_x4

B, I0, I1, I2 = 4096, 128, 8, 4
R1, R2, O2 = 128, 128, 128
FLOPS = 2 * B * (I0 * R1 * I1 * I2 + R1 * I1 * R2 * I2 + R2 * I2 * O2)

P = 128
PACK = 4
HALVES = I1 // PACK
PAIRS = I2 // 2
QUARTERS = HALVES * PAIRS
WORDS = I1 * PAIRS
N_TILES = B // P
COLS = I2 * P
LOOKAHEAD = 5
VECTOR_QUARTERS = 2
GROUP = 4
SORTED_GROUPS = (0, 2)


def rank_order(ap):
    return ap.rearrange("p (a j c d) -> p j a c d", a=4, j=2, c=4, d=4)


def block_order(ap):
    return ap.rearrange("p (a c j d) -> p j a c d", a=4, c=4, j=2, d=4)


def live(n):
    return 0 <= n < N_TILES


def tile_ttmatrix_t_kernel(tc, vector, core0, core1, core2, out):
    nc = tc.nc
    x_dram = vector.rearrange("(n b) i j k -> n b (i j k)", b=P)
    out_dram = out.rearrange("(n b) x y o -> n b (x y o)", b=P)

    with ExitStack() as ctx:
        consts = ctx.enter_context(tc.tile_pool(name="consts", bufs=1))
        x_pool = ctx.enter_context(tc.tile_pool(name="x", bufs=LOOKAHEAD + 1))
        work = ctx.enter_context(tc.tile_pool(name="work", bufs=3))
        xt_psum = ctx.enter_context(tc.psum_pool(name="xt_psum", bufs=3))
        h0_psum = ctx.enter_context(tc.psum_pool(name="h0_psum", bufs=3))
        h1_psum = ctx.enter_context(tc.psum_pool(name="h1_psum", bufs=1))
        out_psum = ctx.enter_context(tc.psum_pool(name="out_psum", bufs=1))
        ctx.enter_context(tc.manual_schedule())

        x_tiles, sorted_tiles, xt_tiles, h0_tiles = {}, {}, {}, {}
        h0_codes, h0_scales, h1_tiles, h1_codes, h1_scales, out_banks = {}, {}, {}, {}, {}, {}

        def load(n):
            if live(n):
                x_sb = x_pool.tile([P, I0 * I1 * I2], BF16)
                nc.sync.dma_start(out=x_sb[:], in_=x_dram[n])
                x_tiles[n] = x_sb

        def sort_words(n):
            if live(n):
                sorted_sb = work.tile([P, len(SORTED_GROUPS) * GROUP, I0], F32)
                x_words = x_tiles[n][:].bitcast(F32).rearrange("b (i w) -> b i w", w=WORDS)
                for j, g in enumerate(SORTED_GROUPS):
                    nc.vector.tensor_copy(
                        out=sorted_sb[:, j * GROUP : (j + 1) * GROUP, :].rearrange("b w i -> b i w"),
                        in_=x_words[:, :, g * GROUP : (g + 1) * GROUP],
                    )
                sorted_tiles[n] = sorted_sb

        load(0)
        c0_sb = consts.tile([P, R1], BF16)
        nc.sync.dma_start(out=c0_sb[:], in_=core0.rearrange("x y i r -> (x y i) r"))
        c1_sb = consts.tile([P, I1 * R2], BF16)
        nc.sync.dma_start(out=c1_sb[:], in_=core1.rearrange("r x i s -> r (x i s)"))
        c2_sb = consts.tile([P, O2 * I2], BF16, align_bytes=64)
        nc.sync.dma_start(out=c2_sb[:], in_=core2.rearrange("r o i x -> r (o i x)"))
        for n in range(1, LOOKAHEAD):
            load(n)

        ident = consts.tile([P, P], F32)
        make_identity(nc, ident[:])
        to_block_order = consts.tile([P, P], BF16)
        for j in range(2):
            nc.vector.tensor_copy(out=block_order(to_block_order[:])[:, j], in_=rank_order(ident[:])[:, j])

        c0_blocked = consts.tile([P, R1], BF16)
        c1_grouped = consts.tile([P, HALVES, R2 * PACK], BF16, align_bytes=64)
        c1_codes = consts.tile([P, HALVES, R2], U32, align_bytes=64)
        c1_scales = consts.tile([P, HALVES, R2], U8, align_bytes=64)
        c2_codes = consts.tile([P, O2], U32, align_bytes=64)
        c2_scales = consts.tile([P, O2], U8, align_bytes=64)

        def prepare_core0():
            for j in range(2):
                nc.vector.tensor_copy(out=block_order(c0_blocked[:])[:, j], in_=rank_order(c0_sb[:])[:, j])

        def prepare_core1_and_core2():
            for h in range(HALVES):
                xt_bank = xt_psum.tile([P, PACK, P], F32)
                nc.tensor.matmul(
                    out=xt_bank[:].rearrange("p t s -> p (t s)"),
                    lhsT=to_block_order[:],
                    rhs=c1_sb[:, h * PACK * R2 : (h + 1) * PACK * R2],
                    start=True,
                    stop=True,
                )
                nc.vector.tensor_copy(
                    out=c1_grouped[:, h, :].rearrange("p (s t) -> p s t", t=PACK),
                    in_=xt_bank[:].rearrange("p t s -> p s t"),
                )
            nc.vector.quantize_mx(out=c2_codes[:].bitcast(FP8X4), scales=c2_scales[:], in_=c2_sb[:])
            nc.vector.quantize_mx(
                out=c1_codes[:].rearrange("p h s -> p (h s)").bitcast(FP8X4),
                scales=c1_scales[:].rearrange("p h s -> p (h s)"),
                in_=c1_grouped[:].rearrange("p h c -> p (h c)"),
            )

        def quarter(n, q, between=()):
            h, u = divmod(q, PAIRS)
            if live(n):
                h0_bank = h0_psum.tile([P, 2, P * PACK], BF16)
            for e in range(2):
                if live(n):
                    nc.tensor.matmul(
                        out=h0_bank[:, e, :],
                        lhsT=c0_blocked[:],
                        rhs=xt_tiles[n][:, q, :].rearrange("p (c e) -> p e c", e=2)[:, e, :],
                        start=True,
                        stop=True,
                    )
                if e == 0:
                    for contraction, tile in between:
                        contraction(tile)
            if live(n + 1):
                xt_bank = xt_psum.tile([P, PACK, P], F32)
                x_words = x_tiles[n + 1][:].bitcast(F32).rearrange("b (i w) -> b w i", w=WORDS)
                for t in (2, 3, 0, 1):
                    w = (PACK * h + t) * PAIRS + u
                    g, w_in_group = divmod(w, GROUP)
                    if g in SORTED_GROUPS:
                        words = sorted_tiles[n + 1][:, SORTED_GROUPS.index(g) * GROUP + w_in_group, :]
                    else:
                        words = x_words[:, w, :]
                    nc.tensor.transpose(out=xt_bank[:, t, :], in_=words, identity=ident[:])
            if live(n):
                width = 2 * P * PACK
                nc.scalar.copy(
                    out=h0_tiles[n][:, h, u * width : (u + 1) * width],
                    in_=h0_bank[:].rearrange("p e c -> p (e c)"),
                )
            if live(n + 1):
                xt_words = xt_tiles[n + 1][:, q, :].bitcast(F32).rearrange("p (b t) -> p b t", t=PACK)
                if q < VECTOR_QUARTERS:
                    nc.vector.tensor_copy(out=xt_words, in_=xt_bank[:].rearrange("p t b -> p b t"))
                else:
                    nc.scalar.copy(out=xt_words, in_=xt_bank[:].rearrange("p t b -> p b t"))

        def quantise_h0(n, h):
            if live(n):
                nc.vector.quantize_mx(
                    out=h0_codes[n][:, h, :].bitcast(FP8X4),
                    scales=h0_scales[n][:, h, :],
                    in_=h0_tiles[n][:, h, :],
                )

        def second_contraction(n):
            if live(n):
                h1_bank = h1_psum.tile([P, COLS], F32)
                for h in range(HALVES):
                    nc.tensor.matmul_mx(
                        out=h1_bank[:],
                        lhsT=c1_codes[:, h, :].bitcast(FP8X4),
                        lhsT_scale=c1_scales[:, h, :],
                        rhs=h0_codes[n][:, h, :].bitcast(FP8X4),
                        rhs_scale=h0_scales[n][:, h, :],
                        start=(h == 0),
                        stop=(h == HALVES - 1),
                    )
                h1_sb = work.tile([P, P, I2], BF16, align_bytes=64)
                nc.scalar.copy(out=h1_sb[:], in_=h1_bank[:].rearrange("p (i b) -> p b i", i=I2))
                h1_tiles[n] = h1_sb

        def quantise_h1(n):
            if live(n):
                codes2 = work.tile([P, P], U32, align_bytes=64)
                scales2 = work.tile([P, P], U8, align_bytes=64)
                nc.vector.quantize_mx(
                    out=codes2[:].bitcast(FP8X4),
                    scales=scales2[:],
                    in_=h1_tiles[n][:].rearrange("p b i -> p (b i)"),
                )
                h1_codes[n], h1_scales[n] = codes2, scales2

        def third_contraction(n):
            if live(n):
                out_bank = out_psum.tile([P, O2], F32)
                nc.tensor.matmul_mx(
                    out=out_bank[:],
                    lhsT=h1_codes[n][:].bitcast(FP8X4),
                    lhsT_scale=h1_scales[n][:],
                    rhs=c2_codes[:].bitcast(FP8X4),
                    rhs_scale=c2_scales[:],
                    start=True,
                    stop=True,
                )
                out_banks[n] = out_bank

        def store(n):
            if live(n):
                result = work.tile([P, O2], F32)
                nc.vector.tensor_copy(out=result[:], in_=out_banks[n][:])
                nc.sync.dma_start(out=out_dram[n], in_=result[:])

        def step(n):
            if live(n):
                h0_sb = work.tile([P, HALVES, COLS * PACK], BF16, align_bytes=64)
                h0_tiles[n] = h0_sb
            if live(n + 1):
                xt_sb = work.tile([P, QUARTERS, P * PACK * 2], BF16)
                xt_tiles[n + 1] = xt_sb
            if live(n - 1):
                codes = work.tile([P, HALVES, COLS], U32, align_bytes=64)
                scales = work.tile([P, HALVES, COLS], U8, align_bytes=64)
                h0_codes[n - 1], h0_scales[n - 1] = codes, scales
            quarter(n, 0)
            quantise_h0(n - 1, 0)
            quarter(n, 1, between=((second_contraction, n - 2), (third_contraction, n - 3)))
            quantise_h0(n - 1, 1)
            quarter(n, 2)
            sort_words(n + 3)
            store(n - 3)
            quarter(n, 3)
            quantise_h1(n - 2)

        sort_words(0)
        prepare_core0()
        sort_words(1)
        step(-1)
        for n in range(N_TILES + 3):
            load(n + LOOKAHEAD)
            step(n)
            if n == 0:
                prepare_core1_and_core2()
